import numpy as np
import ml_dtypes


def mxq(x, axis, fmt="e4m3"):
    dtype, down = {"e4m3": (ml_dtypes.float8_e4m3fn, 7), "e5m2": (ml_dtypes.float8_e5m2, 14)}[fmt]
    v = np.moveaxis(np.asarray(x, np.float32).astype(ml_dtypes.bfloat16).astype(np.float64), axis, -1)
    blocks = v.reshape(v.shape[:-1] + (-1, 32))
    amax = np.abs(blocks).max(-1, keepdims=True)
    byte = np.maximum(np.where(amax > 0, np.frexp(amax)[1] - 1 + 127, 0) - down, 1)
    scale = np.exp2(byte - 127.0)
    codes = (blocks / scale).astype(np.float32).astype(dtype).astype(np.float64)
    return np.moveaxis((codes * scale).reshape(v.shape), -1, axis)


WIDE = False


def mx_kscale(k):
    if not WIDE:
        return np.ones(k)
    levels = np.array([20, -20, 10, -10, 0])
    a = np.random.permutation(np.resize(levels, k // 512 * 4)).reshape(k // 512, 4)
    idx = np.arange(k)
    return np.exp2(a[idx // 512, idx % 128 // 32])


BF16 = ml_dtypes.bfloat16


def bf(x):
    return np.asarray(x, np.float32).astype(BF16)


def f64(x):
    return np.asarray(x).astype(np.float64)


B, D_IN, D_H = 512, 1024, 1024


def sigmoid(v):
    return 1.0 / (1.0 + np.exp(-v))


def setup_inputs():
    s = mx_kscale(B)[:, None]

    def w_in():
        return bf(np.random.standard_normal((D_H, D_IN)) * 0.6 / np.sqrt(D_IN))

    def w_rec():
        return bf(np.random.standard_normal((D_H, D_H)) * 0.6 / np.sqrt(D_H))

    def bias():
        return bf(np.random.standard_normal(D_H) * 0.3)

    x0 = bf(np.random.standard_normal((B, D_IN)))
    h = bf(np.random.standard_normal((B, D_H)))
    W_i = w_in()
    b_W_i = bias()
    W_c = w_in()
    b_W_c = bias()
    U_i = w_rec()
    b_U_i = bias()
    U_c = w_rec()
    b_U_c = bias()
    g = bf(np.random.standard_normal((B, D_H)) * np.exp2(np.random.randint(-12, 1, (B, 1))) * 4.0 / s)
    z_i = f64(x0) @ f64(W_i).T + f64(b_W_i) + f64(h) @ f64(U_i).T + f64(b_U_i)
    C_head = f64(x0) @ f64(W_c).T + f64(b_W_c) + f64(h) @ f64(U_c).T + f64(b_U_c)
    return {"incoming": bf(f64(x0) * s), "h": h,
            "W_i": W_i, "b_W_i": b_W_i, "W_c": W_c, "b_W_c": b_W_c,
            "U_i": U_i, "b_U_i": b_U_i, "U_c": U_c, "b_U_c": b_U_c,
            "z_i": np.asarray(z_i, np.float32), "C_head": np.asarray(C_head, np.float32),
            "grad_out": g}


def reference(incoming, h, W_i, b_W_i, W_c, b_W_c, U_i, b_U_i, U_c, b_U_c, z_i, C_head, grad_out):
    sg = sigmoid(f64(z_i))
    dz = f64(grad_out) * f64(C_head) * (sg * (1.0 - sg))
    return mxq(dz, 0, "e5m2").T @ mxq(f64(incoming), 0, "e4m3")

@@ -1,0 +1,122 @@
+from contextlib import ExitStack
+
+import concourse.mybir as mybir
+
+F32 = mybir.dt.float32
+BF16 = mybir.dt.bfloat16
+U32 = mybir.dt.uint32
+U8 = mybir.dt.uint8
+E4M3X4 = mybir.dt.float8_e4m3fn_x4
+E5M2X4 = mybir.dt.float8_e5m2_x4
+SIGMOID = mybir.ActivationFunctionType.Sigmoid
+MULT = mybir.AluOpType.mult
+
+P = 128
+PACK = 4
+TOKENS = P * PACK
+D_H = 1024
+D_IN = 1024
+M_TILE = 128
+N_TILE = 512
+CHUNK = 256
+RUN = 4
+
+FLOPS = 2 * TOKENS * D_H * D_IN
+BYTES = TOKENS * (D_IN * 2 + D_H * (4 + 4 + 2)) + D_H * D_IN * 4
+
+
+def by_token(tile_ap):
+    return tile_ap.rearrange("p t (c i) -> p c t i", i=RUN)
+
+
+def by_column(tile_ap):
+    return tile_ap.rearrange("p (c i) t -> p c t i", i=RUN)
+
+
+def tile_lstmcell_pa_v_kernel(
+    tc, incoming, h, W_i, b_W_i, W_c, b_W_c, U_i, b_U_i, U_c, b_U_c, z_i, C_head, grad_out, out
+):
+    nc = tc.nc
+    n_chunks = D_H // CHUNK
+
+    x_rows = incoming.rearrange("(p t) w -> p t w", t=PACK)
+    z_rows = z_i.rearrange("(p t) w -> p t w", t=PACK)
+    c_rows = C_head.rearrange("(p t) w -> p t w", t=PACK)
+    g_rows = grad_out.rearrange("(p t) w -> p t w", t=PACK)
+
+    with ExitStack() as ctx:
+        keep = ctx.enter_context(tc.tile_pool(name="keep", bufs=1))
+        chunks = ctx.enter_context(tc.tile_pool(name="chunks", bufs=n_chunks))
+        results = ctx.enter_context(tc.tile_pool(name="results", bufs=D_H // M_TILE))
+        psum = ctx.enter_context(tc.psum_pool(name="psum", bufs=8))
+
+        x_raw = keep.tile([P, PACK, D_IN], BF16)
+        z_tiles, c_tiles, g_tiles = [], [], []
+        for k in range(n_chunks):
+            cols = slice(k * CHUNK, (k + 1) * CHUNK)
+            z_raw = chunks.tile([P, PACK, CHUNK], F32)
+            nc.sync.dma_start(out=z_raw[:], in_=z_rows[:, :, cols])
+            if k == 0:
+                nc.sync.dma_start(out=x_raw[:], in_=x_rows)
+            c_raw = chunks.tile([P, PACK, CHUNK], F32)
+            nc.sync.dma_start(out=c_raw[:], in_=c_rows[:, :, cols])
+            g_raw = chunks.tile([P, PACK, CHUNK], BF16)
+            nc.sync.dma_start(out=g_raw[:], in_=g_rows[:, :, cols])
+            z_tiles.append(z_raw)
+            c_tiles.append(c_raw)
+            g_tiles.append(g_raw)
+
+        x_grouped = keep.tile([P, D_IN, PACK], BF16, align_bytes=64)
+        x_codes = keep.tile([P, D_IN], U32, align_bytes=64)
+        x_scales = keep.tile([P, D_IN], U8, align_bytes=64)
+        for n in range(D_IN // N_TILE):
+            cols = slice(n * N_TILE, (n + 1) * N_TILE)
+            nc.vector.tensor_copy(out=by_column(x_grouped[:, cols, :]), in_=by_token(x_raw[:, :, cols]))
+        for n in range(D_IN // N_TILE):
+            cols = slice(n * N_TILE, (n + 1) * N_TILE)
+            nc.vector.quantize_mx(
+                out=x_codes[:, cols].bitcast(E4M3X4),
+                scales=x_scales[:, cols],
+                in_=x_grouped[:, cols, :].rearrange("p w t -> p (w t)"),
+            )
+
+        for k in range(n_chunks):
+            z_raw, c_raw, g_raw = z_tiles[k], c_tiles[k], g_tiles[k]
+
+            sig_pos = chunks.tile([P, PACK, CHUNK], F32)
+            nc.scalar.activation(out=sig_pos[:], in_=z_raw[:], func=SIGMOID)
+            sig_neg = chunks.tile([P, PACK, CHUNK], F32)
+            nc.scalar.activation(out=sig_neg[:], in_=z_raw[:], func=SIGMOID, scale=-1.0)
+
+            nc.vector.tensor_tensor(out=c_raw[:], in0=c_raw[:], in1=g_raw[:], op=MULT)
+            nc.vector.tensor_tensor(out=sig_pos[:], in0=sig_pos[:], in1=sig_neg[:], op=MULT)
+            dz_grouped = chunks.tile([P, CHUNK, PACK], BF16, align_bytes=64)
+            nc.vector.tensor_tensor(
+                out=by_column(dz_grouped[:]), in0=by_token(c_raw[:]), in1=by_token(sig_pos[:]), op=MULT
+            )
+            dz_codes = chunks.tile([P, CHUNK], U32, align_bytes=64)
+            dz_scales = chunks.tile([P, CHUNK], U8, align_bytes=64)
+            nc.vector.quantize_mx(
+                out=dz_codes[:].bitcast(E5M2X4),
+                scales=dz_scales[:],
+                in_=dz_grouped[:].rearrange("p w t -> p (w t)"),
+            )
+
+            for m in range(CHUNK // M_TILE):
+                m_cols = slice(m * M_TILE, (m + 1) * M_TILE)
+                result = results.tile([P, D_IN], F32)
+                for n in range(D_IN // N_TILE):
+                    n_cols = slice(n * N_TILE, (n + 1) * N_TILE)
+                    acc = psum.tile([M_TILE, N_TILE], F32)
+                    nc.tensor.matmul_mx(
+                        out=acc[:],
+                        lhsT=dz_codes[:, m_cols].bitcast(E5M2X4),
+                        lhsT_scale=dz_scales[:, m_cols],
+                        rhs=x_codes[:, n_cols].bitcast(E4M3X4),
+                        rhs_scale=x_scales[:, n_cols],
+                        start=True,
+                        stop=True,
+                    )
+                    nc.scalar.copy(out=result[:, n_cols], in_=acc[:])
+                row0 = k * CHUNK + m * M_TILE
+                nc.sync.dma_start(out=out[row0 : row0 + M_TILE, :], in_=result[:])

@@ -8,8 +8,8 @@ U32 = mybir.dt.uint32
 U8 = mybir.dt.uint8
 E4M3X4 = mybir.dt.float8_e4m3fn_x4
 E5M2X4 = mybir.dt.float8_e5m2_x4
-SIGMOID = mybir.ActivationFunctionType.Sigmoid
-MULT = mybir.AluOpType.mult
+ACT = mybir.ActivationFunctionType
+ALU = mybir.AluOpType
 
 P = 128
 PACK = 4
@@ -19,6 +19,8 @@ D_IN = 1024
 M_TILE = 128
 N_TILE = 512
 CHUNK = 256
+N_CHUNKS = D_H // CHUNK
+N_HALVES = D_IN // N_TILE
 RUN = 4
 
 FLOPS = 2 * TOKENS * D_H * D_IN
@@ -37,7 +39,6 @@ def tile_lstmcell_pa_v_kernel(
     tc, incoming, h, W_i, b_W_i, W_c, b_W_c, U_i, b_U_i, U_c, b_U_c, z_i, C_head, grad_out, out
 ):
     nc = tc.nc
-    n_chunks = D_H // CHUNK
 
     x_rows = incoming.rearrange("(p t) w -> p t w", t=PACK)
     z_rows = z_i.rearrange("(p t) w -> p t w", t=PACK)
@@ -45,78 +46,118 @@ def tile_lstmcell_pa_v_kernel(
     g_rows = grad_out.rearrange("(p t) w -> p t w", t=PACK)
 
     with ExitStack() as ctx:
+        ctx.enter_context(tc.manual_schedule())
         keep = ctx.enter_context(tc.tile_pool(name="keep", bufs=1))
-        chunks = ctx.enter_context(tc.tile_pool(name="chunks", bufs=n_chunks))
+        chunks = ctx.enter_context(tc.tile_pool(name="chunks", bufs=N_CHUNKS))
         results = ctx.enter_context(tc.tile_pool(name="results", bufs=D_H // M_TILE))
         psum = ctx.enter_context(tc.psum_pool(name="psum", bufs=8))
 
-        x_raw = keep.tile([P, PACK, D_IN], BF16)
-        z_tiles, c_tiles, g_tiles = [], [], []
-        for k in range(n_chunks):
-            cols = slice(k * CHUNK, (k + 1) * CHUNK)
-            z_raw = chunks.tile([P, PACK, CHUNK], F32)
-            nc.sync.dma_start(out=z_raw[:], in_=z_rows[:, :, cols])
-            if k == 0:
-                nc.sync.dma_start(out=x_raw[:], in_=x_rows)
-            c_raw = chunks.tile([P, PACK, CHUNK], F32)
-            nc.sync.dma_start(out=c_raw[:], in_=c_rows[:, :, cols])
-            g_raw = chunks.tile([P, PACK, CHUNK], BF16)
-            nc.sync.dma_start(out=g_raw[:], in_=g_rows[:, :, cols])
-            z_tiles.append(z_raw)
-            c_tiles.append(c_raw)
-            g_tiles.append(g_raw)
-
+        x_tiles = {}
         x_grouped = keep.tile([P, D_IN, PACK], BF16, align_bytes=64)
         x_codes = keep.tile([P, D_IN], U32, align_bytes=64)
         x_scales = keep.tile([P, D_IN], U8, align_bytes=64)
-        for n in range(D_IN // N_TILE):
-            cols = slice(n * N_TILE, (n + 1) * N_TILE)
-            nc.vector.tensor_copy(out=by_column(x_grouped[:, cols, :]), in_=by_token(x_raw[:, :, cols]))
-        for n in range(D_IN // N_TILE):
-            cols = slice(n * N_TILE, (n + 1) * N_TILE)
-            nc.vector.quantize_mx(
-                out=x_codes[:, cols].bitcast(E4M3X4),
-                scales=x_scales[:, cols],
-                in_=x_grouped[:, cols, :].rearrange("p w t -> p (w t)"),
+        z_tiles, c_tiles, g_tiles, slope_tiles, code_tiles, scale_tiles, acc_tiles = {}, {}, {}, {}, {}, {}, {}
+
+        def chunk_cols(k):
+            return slice(k * CHUNK, (k + 1) * CHUNK)
+
+        def half_cols(n):
+            return slice(n * N_TILE, (n + 1) * N_TILE)
+
+        def load_z(k):
+            z_tiles[k] = chunks.tile([P, PACK, CHUNK], F32, name="z_raw")
+            nc.sync.dma_start(out=z_tiles[k][:], in_=z_rows[:, :, chunk_cols(k)])
+
+        def load_x(n):
+            x_tiles[n] = keep.tile([P, PACK, N_TILE], BF16, name="x_raw%d" % n)
+            nc.sync.dma_start(out=x_tiles[n][:], in_=x_rows[:, :, half_cols(n)])
+
+        def load_g_and_c(k):
+            g_tiles[k] = chunks.tile([P, PACK, CHUNK], BF16, name="g_raw")
+            nc.sync.dma_start(out=g_tiles[k][:], in_=g_rows[:, :, chunk_cols(k)])
+            c_tiles[k] = chunks.tile([P, PACK, CHUNK], F32, name="c_raw")
+            nc.sync.dma_start(out=c_tiles[k][:], in_=c_rows[:, :, chunk_cols(k)])
+
+        def gate(k):
+            sig = chunks.tile([P, PACK, CHUNK], F32, name="sig")
+            nc.scalar.activation(out=sig[:], in_=z_tiles[k][:], func=ACT.Sigmoid)
+            slope_tiles[k] = chunks.tile([P, PACK, CHUNK], F32, name="slope")
+            nc.scalar.activation(out=slope_tiles[k][:], in_=sig[:], func=ACT.Square, bias=-0.5)
+
+        def prepare_x():
+            for n in range(N_HALVES):
+                cols = half_cols(n)
+                nc.vector.tensor_copy(out=by_column(x_grouped[:, cols, :]), in_=by_token(x_tiles[n][:]))
+            for n in range(N_HALVES):
+                cols = half_cols(n)
+                nc.vector.quantize_mx(
+                    out=x_codes[:, cols].bitcast(E4M3X4),
+                    scales=x_scales[:, cols],
+                    in_=x_grouped[:, cols, :].rearrange("p w t -> p (w t)"),
+                )
+
+        def products(k):
+            slope = slope_tiles[k]
+            nc.vector.scalar_tensor_tensor(
+                out=slope[:], in0=slope[:], scalar=0.25, in1=g_tiles[k][:],
+                op0=ALU.subtract, op1=ALU.mult,
             )
-
-        for k in range(n_chunks):
-            z_raw, c_raw, g_raw = z_tiles[k], c_tiles[k], g_tiles[k]
-
-            sig_pos = chunks.tile([P, PACK, CHUNK], F32)
-            nc.scalar.activation(out=sig_pos[:], in_=z_raw[:], func=SIGMOID)
-            sig_neg = chunks.tile([P, PACK, CHUNK], F32)
-            nc.scalar.activation(out=sig_neg[:], in_=z_raw[:], func=SIGMOID, scale=-1.0)
-
-            nc.vector.tensor_tensor(out=c_raw[:], in0=c_raw[:], in1=g_raw[:], op=MULT)
-            nc.vector.tensor_tensor(out=sig_pos[:], in0=sig_pos[:], in1=sig_neg[:], op=MULT)
-            dz_grouped = chunks.tile([P, CHUNK, PACK], BF16, align_bytes=64)
+            dz_grouped = chunks.tile([P, CHUNK, PACK], BF16, align_bytes=64, name="dz_grouped")
             nc.vector.tensor_tensor(
-                out=by_column(dz_grouped[:]), in0=by_token(c_raw[:]), in1=by_token(sig_pos[:]), op=MULT
+                out=by_column(dz_grouped[:]), in0=by_token(slope[:]), in1=by_token(c_tiles[k][:]), op=ALU.mult
             )
-            dz_codes = chunks.tile([P, CHUNK], U32, align_bytes=64)
-            dz_scales = chunks.tile([P, CHUNK], U8, align_bytes=64)
+            code_tiles[k] = chunks.tile([P, CHUNK], U32, align_bytes=64, name="dz_codes")
+            scale_tiles[k] = chunks.tile([P, CHUNK], U8, align_bytes=64, name="dz_scales")
             nc.vector.quantize_mx(
-                out=dz_codes[:].bitcast(E5M2X4),
-                scales=dz_scales[:],
+                out=code_tiles[k][:].bitcast(E5M2X4),
+                scales=scale_tiles[k][:],
                 in_=dz_grouped[:].rearrange("p w t -> p (w t)"),
             )
 
+        def multiply(k):
             for m in range(CHUNK // M_TILE):
                 m_cols = slice(m * M_TILE, (m + 1) * M_TILE)
-                result = results.tile([P, D_IN], F32)
-                for n in range(D_IN // N_TILE):
-                    n_cols = slice(n * N_TILE, (n + 1) * N_TILE)
-                    acc = psum.tile([M_TILE, N_TILE], F32)
+                for n in range(N_HALVES):
+                    acc_tiles[k, m, n] = psum.tile([M_TILE, N_TILE], F32, name="acc")
                     nc.tensor.matmul_mx(
-                        out=acc[:],
-                        lhsT=dz_codes[:, m_cols].bitcast(E5M2X4),
-                        lhsT_scale=dz_scales[:, m_cols],
-                        rhs=x_codes[:, n_cols].bitcast(E4M3X4),
-                        rhs_scale=x_scales[:, n_cols],
+                        out=acc_tiles[k, m, n][:],
+                        lhsT=code_tiles[k][:, m_cols].bitcast(E5M2X4),
+                        lhsT_scale=scale_tiles[k][:, m_cols],
+                        rhs=x_codes[:, half_cols(n)].bitcast(E4M3X4),
+                        rhs_scale=x_scales[:, half_cols(n)],
                         start=True,
                         stop=True,
                     )
-                    nc.scalar.copy(out=result[:, n_cols], in_=acc[:])
+
+        def empty_and_store(k):
+            vector_helps = k == N_CHUNKS - 1
+            for m in range(CHUNK // M_TILE):
+                result = results.tile([P, D_IN], F32, name="result")
+                for n in range(N_HALVES):
+                    if vector_helps and n == 1:
+                        nc.vector.tensor_scalar_mul(out=result[:, half_cols(n)], in0=acc_tiles[k, m, n][:], scalar1=-1.0)
+                    else:
+                        nc.scalar.mul(out=result[:, half_cols(n)], in_=acc_tiles[k, m, n][:], mul=-1.0)
                 row0 = k * CHUNK + m * M_TILE
                 nc.sync.dma_start(out=out[row0 : row0 + M_TILE, :], in_=result[:])
+
+        load_z(0)
+        load_x(0)
+        load_z(1)
+        load_x(1)
+        for k in range(N_CHUNKS):
+            if k + 2 < N_CHUNKS:
+                load_z(k + 2)
+            load_g_and_c(k)
+
+        gate(0)
+        prepare_x()
+        gate(1)
+        for k in range(N_CHUNKS):
+            if k + 2 < N_CHUNKS:
+                gate(k + 2)
+            products(k)
+            multiply(k)
+            if k >= 1:
+                empty_and_store(k - 1)
+        empty_and_store(N_CHUNKS - 1)

@@ -10,6 +10,7 @@ E4M3X4 = mybir.dt.float8_e4m3fn_x4
 E5M2X4 = mybir.dt.float8_e5m2_x4
 ACT = mybir.ActivationFunctionType
 ALU = mybir.AluOpType
+ENG = mybir.EngineType
 
 P = 128
 PACK = 4
@@ -18,13 +19,18 @@ D_H = 1024
 D_IN = 1024
 M_TILE = 128
 N_TILE = 512
-CHUNK = 256
-N_CHUNKS = D_H // CHUNK
 N_HALVES = D_IN // N_TILE
 RUN = 4
 
 FLOPS = 2 * TOKENS * D_H * D_IN
 BYTES = TOKENS * (D_IN * 2 + D_H * (4 + 4 + 2)) + D_H * D_IN * 4
+
+LOADS = [("z", 0, 256), ("x", 0, 512), ("z", 256, 256), ("x", 512, 512), ("z", 512, 256), ("g", 0, 256), ("c", 0, 256),
+         ("z", 768, 256), ("g", 256, 256), ("c", 256, 256), ("g", 512, 256), ("c", 512, 256), ("g", 768, 256), ("c", 768, 256)]
+CHUNKS = [(0, 256), (256, 256), (512, 256), (768, 256)]
+SPLIT_STORES = []
+PINNED = "all"
+ORDER = "G0 X0 G1 X1 Y0 G2 S0 Y1 T0 G3 S1 Q0 M0 T1 S2 Q1 M1 A000 A001 A010 A011 T2 S3 Q2 M2 A100 A101 A110 A111 T3 Q3 M3 A200 V201 A210 V211 A300 V301 A310 V311"
 
 
 def by_token(tile_ap):
@@ -39,125 +45,138 @@ def tile_lstmcell_pa_v_kernel(
     tc, incoming, h, W_i, b_W_i, W_c, b_W_c, U_i, b_U_i, U_c, b_U_c, z_i, C_head, grad_out, out
 ):
     nc = tc.nc
-
-    x_rows = incoming.rearrange("(p t) w -> p t w", t=PACK)
-    z_rows = z_i.rearrange("(p t) w -> p t w", t=PACK)
-    c_rows = C_head.rearrange("(p t) w -> p t w", t=PACK)
-    g_rows = grad_out.rearrange("(p t) w -> p t w", t=PACK)
+    rows = {
+        "x": incoming.rearrange("(p t) w -> p t w", t=PACK),
+        "z": z_i.rearrange("(p t) w -> p t w", t=PACK),
+        "c": C_head.rearrange("(p t) w -> p t w", t=PACK),
+        "g": grad_out.rearrange("(p t) w -> p t w", t=PACK),
+    }
+    dtypes = {"x": BF16, "z": F32, "c": F32, "g": BF16}
 
     with ExitStack() as ctx:
-        ctx.enter_context(tc.manual_schedule())
+        if PINNED == "all":
+            ctx.enter_context(tc.manual_schedule())
+        elif PINNED == "some":
+            ctx.enter_context(tc.manual_schedule(engines={ENG.SP, ENG.PE}))
         keep = ctx.enter_context(tc.tile_pool(name="keep", bufs=1))
-        chunks = ctx.enter_context(tc.tile_pool(name="chunks", bufs=N_CHUNKS))
-        results = ctx.enter_context(tc.tile_pool(name="results", bufs=D_H // M_TILE))
         psum = ctx.enter_context(tc.psum_pool(name="psum", bufs=8))
 
-        x_tiles = {}
-        x_grouped = keep.tile([P, D_IN, PACK], BF16, align_bytes=64)
-        x_codes = keep.tile([P, D_IN], U32, align_bytes=64)
-        x_scales = keep.tile([P, D_IN], U8, align_bytes=64)
-        z_tiles, c_tiles, g_tiles, slope_tiles, code_tiles, scale_tiles, acc_tiles = {}, {}, {}, {}, {}, {}, {}
-
-        def chunk_cols(k):
-            return slice(k * CHUNK, (k + 1) * CHUNK)
+        pieces = []
+        x_grouped = keep.tile([P, D_IN, PACK], BF16, align_bytes=64, name="x_grouped")
+        x_codes = keep.tile([P, D_IN], U32, align_bytes=64, name="x_codes")
+        x_scales = keep.tile([P, D_IN], U8, align_bytes=64, name="x_scales")
+        sig, slope, grouped, codes, scales, acc, result, emptied = {}, {}, {}, {}, {}, {}, {}, {}
 
         def half_cols(n):
             return slice(n * N_TILE, (n + 1) * N_TILE)
 
-        def load_z(k):
-            z_tiles[k] = chunks.tile([P, PACK, CHUNK], F32, name="z_raw")
-            nc.sync.dma_start(out=z_tiles[k][:], in_=z_rows[:, :, chunk_cols(k)])
+        def load(tensor, c0, w):
+            t = keep.tile([P, PACK, w], dtypes[tensor], name="%s_raw_%d" % (tensor, c0))
+            nc.sync.dma_start(out=t[:], in_=rows[tensor][:, :, c0 : c0 + w])
+            pieces.append((tensor, c0, w, t))
 
-        def load_x(n):
-            x_tiles[n] = keep.tile([P, PACK, N_TILE], BF16, name="x_raw%d" % n)
-            nc.sync.dma_start(out=x_tiles[n][:], in_=x_rows[:, :, half_cols(n)])
-
-        def load_g_and_c(k):
-            g_tiles[k] = chunks.tile([P, PACK, CHUNK], BF16, name="g_raw")
-            nc.sync.dma_start(out=g_tiles[k][:], in_=g_rows[:, :, chunk_cols(k)])
-            c_tiles[k] = chunks.tile([P, PACK, CHUNK], F32, name="c_raw")
-            nc.sync.dma_start(out=c_tiles[k][:], in_=c_rows[:, :, chunk_cols(k)])
+        def raw(tensor, c0, w):
+            for (name, p0, pw, t) in pieces:
+                if name == tensor and p0 <= c0 and c0 + w <= p0 + pw:
+                    return t[:, :, c0 - p0 : c0 - p0 + w]
+            raise ValueError("no piece holds %s %d %d" % (tensor, c0, w))
 
         def gate(k):
-            sig = chunks.tile([P, PACK, CHUNK], F32, name="sig")
-            nc.scalar.activation(out=sig[:], in_=z_tiles[k][:], func=ACT.Sigmoid)
-            slope_tiles[k] = chunks.tile([P, PACK, CHUNK], F32, name="slope")
-            nc.scalar.activation(out=slope_tiles[k][:], in_=sig[:], func=ACT.Square, bias=-0.5)
+            c0, w = CHUNKS[k]
+            sig[k] = keep.tile([P, PACK, w], F32, name="sig%d" % k)
+            nc.scalar.activation(out=sig[k][:], in_=raw("z", c0, w), func=ACT.Sigmoid)
+            slope[k] = keep.tile([P, PACK, w], F32, name="slope%d" % k)
+            nc.scalar.activation(out=slope[k][:], in_=sig[k][:], func=ACT.Square, bias=-0.5)
 
-        def prepare_x():
-            for n in range(N_HALVES):
-                cols = half_cols(n)
-                nc.vector.tensor_copy(out=by_column(x_grouped[:, cols, :]), in_=by_token(x_tiles[n][:]))
-            for n in range(N_HALVES):
-                cols = half_cols(n)
-                nc.vector.quantize_mx(
-                    out=x_codes[:, cols].bitcast(E4M3X4),
-                    scales=x_scales[:, cols],
-                    in_=x_grouped[:, cols, :].rearrange("p w t -> p (w t)"),
-                )
+        def x_copy(n):
+            cols = half_cols(n)
+            nc.vector.tensor_copy(out=by_column(x_grouped[:, cols, :]), in_=by_token(raw("x", n * N_TILE, N_TILE)))
 
-        def products(k):
-            slope = slope_tiles[k]
+        def x_quant(n):
+            cols = half_cols(n)
+            nc.vector.quantize_mx(
+                out=x_codes[:, cols].bitcast(E4M3X4),
+                scales=x_scales[:, cols],
+                in_=x_grouped[:, cols, :].rearrange("p w t -> p (w t)"),
+            )
+
+        def first_product(k):
+            c0, w = CHUNKS[k]
             nc.vector.scalar_tensor_tensor(
-                out=slope[:], in0=slope[:], scalar=0.25, in1=g_tiles[k][:],
+                out=slope[k][:], in0=slope[k][:], scalar=0.25, in1=raw("g", c0, w),
                 op0=ALU.subtract, op1=ALU.mult,
             )
-            dz_grouped = chunks.tile([P, CHUNK, PACK], BF16, align_bytes=64, name="dz_grouped")
+
+        def second_product(k):
+            c0, w = CHUNKS[k]
+            grouped[k] = keep.tile([P, w, PACK], BF16, align_bytes=64, name="grouped%d" % k)
             nc.vector.tensor_tensor(
-                out=by_column(dz_grouped[:]), in0=by_token(slope[:]), in1=by_token(c_tiles[k][:]), op=ALU.mult
+                out=by_column(grouped[k][:]), in0=by_token(slope[k][:]), in1=by_token(raw("c", c0, w)), op=ALU.mult
             )
-            code_tiles[k] = chunks.tile([P, CHUNK], U32, align_bytes=64, name="dz_codes")
-            scale_tiles[k] = chunks.tile([P, CHUNK], U8, align_bytes=64, name="dz_scales")
+
+        def quant(k):
+            c0, w = CHUNKS[k]
+            codes[k] = keep.tile([P, w], U32, align_bytes=64, name="codes%d" % k)
+            scales[k] = keep.tile([P, w], U8, align_bytes=64, name="scales%d" % k)
             nc.vector.quantize_mx(
-                out=code_tiles[k][:].bitcast(E5M2X4),
-                scales=scale_tiles[k][:],
-                in_=dz_grouped[:].rearrange("p w t -> p (w t)"),
+                out=codes[k][:].bitcast(E5M2X4),
+                scales=scales[k][:],
+                in_=grouped[k][:].rearrange("p w t -> p (w t)"),
             )
 
         def multiply(k):
-            for m in range(CHUNK // M_TILE):
+            c0, w = CHUNKS[k]
+            for m in range(w // M_TILE):
                 m_cols = slice(m * M_TILE, (m + 1) * M_TILE)
                 for n in range(N_HALVES):
-                    acc_tiles[k, m, n] = psum.tile([M_TILE, N_TILE], F32, name="acc")
+                    acc[k, m, n] = psum.tile([M_TILE, N_TILE], F32, name="acc")
                     nc.tensor.matmul_mx(
-                        out=acc_tiles[k, m, n][:],
-                        lhsT=code_tiles[k][:, m_cols].bitcast(E5M2X4),
-                        lhsT_scale=scale_tiles[k][:, m_cols],
+                        out=acc[k, m, n][:],
+                        lhsT=codes[k][:, m_cols].bitcast(E5M2X4),
+                        lhsT_scale=scales[k][:, m_cols],
                         rhs=x_codes[:, half_cols(n)].bitcast(E4M3X4),
                         rhs_scale=x_scales[:, half_cols(n)],
                         start=True,
                         stop=True,
                     )
 
-        def empty_and_store(k):
-            vector_helps = k == N_CHUNKS - 1
-            for m in range(CHUNK // M_TILE):
-                result = results.tile([P, D_IN], F32, name="result")
-                for n in range(N_HALVES):
-                    if vector_helps and n == 1:
-                        nc.vector.tensor_scalar_mul(out=result[:, half_cols(n)], in0=acc_tiles[k, m, n][:], scalar1=-1.0)
-                    else:
-                        nc.scalar.mul(out=result[:, half_cols(n)], in_=acc_tiles[k, m, n][:], mul=-1.0)
-                row0 = k * CHUNK + m * M_TILE
-                nc.sync.dma_start(out=out[row0 : row0 + M_TILE, :], in_=result[:])
+        def empty(who, k, m, n):
+            c0, w = CHUNKS[k]
+            if (k, m) not in result:
+                result[k, m] = keep.tile([P, D_IN], F32, name="result%d_%d" % (k, m))
+                emptied[k, m] = 0
+            dst = result[k, m][:, half_cols(n)]
+            if who == "A":
+                nc.scalar.mul(out=dst, in_=acc[k, m, n][:], mul=-1.0)
+            elif who == "V":
+                nc.vector.tensor_scalar_mul(out=dst, in0=acc[k, m, n][:], scalar1=-1.0)
+            else:
+                nc.any.tensor_scalar_mul(out=dst, in0=acc[k, m, n][:], scalar1=-1.0)
+            emptied[k, m] = emptied[k, m] + 1
+            row0 = c0 + m * M_TILE
+            if (k, m) in SPLIT_STORES:
+                nc.sync.dma_start(out=out[row0 : row0 + M_TILE, half_cols(n)], in_=dst)
+            elif emptied[k, m] == N_HALVES:
+                nc.sync.dma_start(out=out[row0 : row0 + M_TILE, :], in_=result[k, m][:])
 
-        load_z(0)
-        load_x(0)
-        load_z(1)
-        load_x(1)
-        for k in range(N_CHUNKS):
-            if k + 2 < N_CHUNKS:
-                load_z(k + 2)
-            load_g_and_c(k)
+        for (tensor, c0, w) in LOADS:
+            load(tensor, c0, w)
 
-        gate(0)
-        prepare_x()
-        gate(1)
-        for k in range(N_CHUNKS):
-            if k + 2 < N_CHUNKS:
-                gate(k + 2)
-            products(k)
-            multiply(k)
-            if k >= 1:
-                empty_and_store(k - 1)
-        empty_and_store(N_CHUNKS - 1)
+        for token in ORDER.split():
+            op = token[0]
+            if op == "G":
+                gate(int(token[1]))
+            elif op == "X":
+                x_copy(int(token[1]))
+            elif op == "Y":
+                x_quant(int(token[1]))
+            elif op == "S":
+                first_product(int(token[1]))
+            elif op == "T":
+                second_product(int(token[1]))
+            elif op == "Q":
+                quant(int(token[1]))
+            elif op == "M":
+                multiply(int(token[1]))
+            else:
+                empty(op, int(token[1]), int(token[2]), int(token[3]))

@@ -30,7 +30,7 @@ LOADS = [("z", 0, 256), ("x", 0, 512), ("z", 256, 256), ("x", 512, 512), ("z", 5
 CHUNKS = [(0, 256), (256, 256), (512, 256), (768, 256)]
 SPLIT_STORES = []
 PINNED = "all"
-ORDER = "G0 X0 G1 X1 Y0 G2 S0 Y1 T0 G3 S1 Q0 M0 T1 S2 Q1 M1 A000 A001 A010 A011 T2 S3 Q2 M2 A100 A101 A110 A111 T3 Q3 M3 A200 V201 A210 V211 A300 V301 A310 V311"
+ORDER = "G0 X0 G1 X1 Y0 G2 S0 Y1 T0 G3 S1 Q0 M0 T1 S2 Q1 M1 A000 A001 A010 A011 T2 S3 Q2 M2 A100 A101 A110 A111 T3 Q3 M3 A200 A201 A210 A211 V300 V301 A310 V311"
 
 
 def by_token(tile_ap):

@@ -25,8 +25,8 @@ RUN = 4
 FLOPS = 2 * TOKENS * D_H * D_IN
 BYTES = TOKENS * (D_IN * 2 + D_H * (4 + 4 + 2)) + D_H * D_IN * 4
 
-LOADS = [("z", 0, 256), ("x", 0, 512), ("z", 256, 256), ("x", 512, 512), ("z", 512, 256), ("g", 0, 256), ("c", 0, 256),
-         ("z", 768, 256), ("g", 256, 256), ("c", 256, 256), ("g", 512, 256), ("c", 512, 256), ("g", 768, 256), ("c", 768, 256)]
+LOADS = [("z", 0, 256), ("x", 0, 1024), ("z", 256, 256), ("z", 512, 256), ("g", 0, 512), ("c", 0, 256),
+         ("z", 768, 256), ("c", 256, 256), ("g", 512, 512), ("c", 512, 256), ("c", 768, 256)]
 CHUNKS = [(0, 256), (256, 256), (512, 256), (768, 256)]
 SPLIT_STORES = []
 PINNED = "all"

@@ -25,12 +25,14 @@ RUN = 4
 FLOPS = 2 * TOKENS * D_H * D_IN
 BYTES = TOKENS * (D_IN * 2 + D_H * (4 + 4 + 2)) + D_H * D_IN * 4
 
-LOADS = [("z", 0, 256), ("x", 0, 1024), ("z", 256, 256), ("z", 512, 256), ("g", 0, 512), ("c", 0, 256),
-         ("z", 768, 256), ("c", 256, 256), ("g", 512, 512), ("c", 512, 256), ("c", 768, 256)]
+LOADS = [("z", 0, 256, "sync"), ("x", 0, 1024, "sync"), ("g", 0, 512, "sync"), ("z", 256, 256, "sync"), ("c", 0, 256, "sync"),
+         ("z", 512, 256, "sync"), ("c", 256, 256, "sync"), ("g", 512, 512, "sync"), ("z", 768, 256, "sync"), ("c", 512, 256, "sync"),
+         ("c", 768, 256, "sync")]
 CHUNKS = [(0, 256), (256, 256), (512, 256), (768, 256)]
 SPLIT_STORES = []
+GPSIMD_STORES = []
 PINNED = "all"
-ORDER = "G0 X0 G1 X1 Y0 G2 S0 Y1 T0 G3 S1 Q0 M0 T1 S2 Q1 M1 A000 A001 A010 A011 T2 S3 Q2 M2 A100 A101 A110 A111 T3 Q3 M3 A200 A201 A210 A211 V300 V301 A310 V311"
+ORDER = "G0 X1 W0 S0 Y0 Y1 G1 T0 G2 S1 Q0 M0 T1 S2 Q1 M1 A000 A001 A010 V011 G3 V100 T2 Q2 M2 A101 A110 A111 S3 T3 Q3 M3 A200 A201 A210 A211 V300 A301 V310 A311"
 
 
 def by_token(tile_ap):
@@ -70,9 +72,10 @@ def tile_lstmcell_pa_v_kernel(
         def half_cols(n):
             return slice(n * N_TILE, (n + 1) * N_TILE)
 
-        def load(tensor, c0, w):
+        def load(tensor, c0, w, queue):
             t = keep.tile([P, PACK, w], dtypes[tensor], name="%s_raw_%d" % (tensor, c0))
-            nc.sync.dma_start(out=t[:], in_=rows[tensor][:, :, c0 : c0 + w])
+            engine = nc.sync if queue == "sync" else nc.scalar
+            engine.dma_start(out=t[:], in_=rows[tensor][:, :, c0 : c0 + w])
             pieces.append((tensor, c0, w, t))
 
         def raw(tensor, c0, w):
@@ -91,6 +94,10 @@ def tile_lstmcell_pa_v_kernel(
         def x_copy(n):
             cols = half_cols(n)
             nc.vector.tensor_copy(out=by_column(x_grouped[:, cols, :]), in_=by_token(raw("x", n * N_TILE, N_TILE)))
+
+        def x_copy_on_scalar(n):
+            cols = half_cols(n)
+            nc.scalar.copy(out=by_column(x_grouped[:, cols, :]), in_=by_token(raw("x", n * N_TILE, N_TILE)))
 
         def x_quant(n):
             cols = half_cols(n)
@@ -154,13 +161,14 @@ def tile_lstmcell_pa_v_kernel(
                 nc.any.tensor_scalar_mul(out=dst, in0=acc[k, m, n][:], scalar1=-1.0)
             emptied[k, m] = emptied[k, m] + 1
             row0 = c0 + m * M_TILE
+            store_engine = nc.gpsimd if (k, m) in GPSIMD_STORES else nc.sync
             if (k, m) in SPLIT_STORES:
-                nc.sync.dma_start(out=out[row0 : row0 + M_TILE, half_cols(n)], in_=dst)
+                store_engine.dma_start(out=out[row0 : row0 + M_TILE, half_cols(n)], in_=dst)
             elif emptied[k, m] == N_HALVES:
-                nc.sync.dma_start(out=out[row0 : row0 + M_TILE, :], in_=result[k, m][:])
+                store_engine.dma_start(out=out[row0 : row0 + M_TILE, :], in_=result[k, m][:])
 
-        for (tensor, c0, w) in LOADS:
-            load(tensor, c0, w)
+        for (tensor, c0, w, queue) in LOADS:
+            load(tensor, c0, w, queue)
 
         for token in ORDER.split():
             op = token[0]
@@ -168,6 +176,8 @@ def tile_lstmcell_pa_v_kernel(
                 gate(int(token[1]))
             elif op == "X":
                 x_copy(int(token[1]))
+            elif op == "W":
+                x_copy_on_scalar(int(token[1]))
             elif op == "Y":
                 x_quant(int(token[1]))
             elif op == "S":

from contextlib import ExitStack

import concourse.mybir as mybir

F32 = mybir.dt.float32
BF16 = mybir.dt.bfloat16
U32 = mybir.dt.uint32
U8 = mybir.dt.uint8
E4M3X4 = mybir.dt.float8_e4m3fn_x4
E5M2X4 = mybir.dt.float8_e5m2_x4
ACT = mybir.ActivationFunctionType
ALU = mybir.AluOpType
ENG = mybir.EngineType

P = 128
PACK = 4
TOKENS = P * PACK
D_H = 1024
D_IN = 1024
M_TILE = 128
N_TILE = 512
N_HALVES = D_IN // N_TILE
RUN = 4

FLOPS = 2 * TOKENS * D_H * D_IN
BYTES = TOKENS * (D_IN * 2 + D_H * (4 + 4 + 2)) + D_H * D_IN * 4

LOADS = [("z", 0, 256, "sync"), ("x", 0, 1024, "sync"), ("g", 0, 512, "sync"), ("z", 256, 256, "sync"), ("c", 0, 256, "sync"),
         ("z", 512, 256, "sync"), ("c", 256, 256, "sync"), ("g", 512, 512, "sync"), ("z", 768, 256, "sync"), ("c", 512, 256, "sync"),
         ("c", 768, 256, "sync")]
CHUNKS = [(0, 256), (256, 256), (512, 256), (768, 256)]
SPLIT_STORES = []
GPSIMD_STORES = []
PINNED = "all"
ORDER = "G0 X1 W0 S0 Y0 Y1 G1 T0 G2 S1 Q0 M0 T1 S2 Q1 M1 A000 A001 A010 V011 G3 V100 T2 Q2 M2 A101 A110 A111 S3 T3 Q3 M3 A200 A201 A210 A211 V300 A301 V310 A311"


def by_token(tile_ap):
    return tile_ap.rearrange("p t (c i) -> p c t i", i=RUN)


def by_column(tile_ap):
    return tile_ap.rearrange("p (c i) t -> p c t i", i=RUN)


def tile_lstmcell_pa_v_kernel(
    tc, incoming, h, W_i, b_W_i, W_c, b_W_c, U_i, b_U_i, U_c, b_U_c, z_i, C_head, grad_out, out
):
    nc = tc.nc
    rows = {
        "x": incoming.rearrange("(p t) w -> p t w", t=PACK),
        "z": z_i.rearrange("(p t) w -> p t w", t=PACK),
        "c": C_head.rearrange("(p t) w -> p t w", t=PACK),
        "g": grad_out.rearrange("(p t) w -> p t w", t=PACK),
    }
    dtypes = {"x": BF16, "z": F32, "c": F32, "g": BF16}

    with ExitStack() as ctx:
        if PINNED == "all":
            ctx.enter_context(tc.manual_schedule())
        elif PINNED == "some":
            ctx.enter_context(tc.manual_schedule(engines={ENG.SP, ENG.PE}))
        keep = ctx.enter_context(tc.tile_pool(name="keep", bufs=1))
        psum = ctx.enter_context(tc.psum_pool(name="psum", bufs=8))

        pieces = []
        x_grouped = keep.tile([P, D_IN, PACK], BF16, align_bytes=64, name="x_grouped")
        x_codes = keep.tile([P, D_IN], U32, align_bytes=64, name="x_codes")
        x_scales = keep.tile([P, D_IN], U8, align_bytes=64, name="x_scales")
        sig, slope, grouped, codes, scales, acc, result, emptied = {}, {}, {}, {}, {}, {}, {}, {}

        def half_cols(n):
            return slice(n * N_TILE, (n + 1) * N_TILE)

        def load(tensor, c0, w, queue):
            t = keep.tile([P, PACK, w], dtypes[tensor], name="%s_raw_%d" % (tensor, c0))
            engine = nc.sync if queue == "sync" else nc.scalar
            engine.dma_start(out=t[:], in_=rows[tensor][:, :, c0 : c0 + w])
            pieces.append((tensor, c0, w, t))

        def raw(tensor, c0, w):
            for (name, p0, pw, t) in pieces:
                if name == tensor and p0 <= c0 and c0 + w <= p0 + pw:
                    return t[:, :, c0 - p0 : c0 - p0 + w]
            raise ValueError("no piece holds %s %d %d" % (tensor, c0, w))

        def gate(k):
            c0, w = CHUNKS[k]
            sig[k] = keep.tile([P, PACK, w], F32, name="sig%d" % k)
            nc.scalar.activation(out=sig[k][:], in_=raw("z", c0, w), func=ACT.Sigmoid)
            slope[k] = keep.tile([P, PACK, w], F32, name="slope%d" % k)
            nc.scalar.activation(out=slope[k][:], in_=sig[k][:], func=ACT.Square, bias=-0.5)

        def x_copy(n):
            cols = half_cols(n)
            nc.vector.tensor_copy(out=by_column(x_grouped[:, cols, :]), in_=by_token(raw("x", n * N_TILE, N_TILE)))

        def x_copy_on_scalar(n):
            cols = half_cols(n)
            nc.scalar.copy(out=by_column(x_grouped[:, cols, :]), in_=by_token(raw("x", n * N_TILE, N_TILE)))

        def x_quant(n):
            cols = half_cols(n)
            nc.vector.quantize_mx(
                out=x_codes[:, cols].bitcast(E4M3X4),
                scales=x_scales[:, cols],
                in_=x_grouped[:, cols, :].rearrange("p w t -> p (w t)"),
            )

        def first_product(k):
            c0, w = CHUNKS[k]
            nc.vector.scalar_tensor_tensor(
                out=slope[k][:], in0=slope[k][:], scalar=0.25, in1=raw("g", c0, w),
                op0=ALU.subtract, op1=ALU.mult,
            )

        def second_product(k):
            c0, w = CHUNKS[k]
            grouped[k] = keep.tile([P, w, PACK], BF16, align_bytes=64, name="grouped%d" % k)
            nc.vector.tensor_tensor(
                out=by_column(grouped[k][:]), in0=by_token(slope[k][:]), in1=by_token(raw("c", c0, w)), op=ALU.mult
            )

        def quant(k):
            c0, w = CHUNKS[k]
            codes[k] = keep.tile([P, w], U32, align_bytes=64, name="codes%d" % k)
            scales[k] = keep.tile([P, w], U8, align_bytes=64, name="scales%d" % k)
            nc.vector.quantize_mx(
                out=codes[k][:].bitcast(E5M2X4),
                scales=scales[k][:],
                in_=grouped[k][:].rearrange("p w t -> p (w t)"),
            )

        def multiply(k):
            c0, w = CHUNKS[k]
            for m in range(w // M_TILE):
                m_cols = slice(m * M_TILE, (m + 1) * M_TILE)
                for n in range(N_HALVES):
                    acc[k, m, n] = psum.tile([M_TILE, N_TILE], F32, name="acc")
                    nc.tensor.matmul_mx(
                        out=acc[k, m, n][:],
                        lhsT=codes[k][:, m_cols].bitcast(E5M2X4),
                        lhsT_scale=scales[k][:, m_cols],
                        rhs=x_codes[:, half_cols(n)].bitcast(E4M3X4),
                        rhs_scale=x_scales[:, half_cols(n)],
                        start=True,
                        stop=True,
                    )

        def empty(who, k, m, n):
            c0, w = CHUNKS[k]
            if (k, m) not in result:
                result[k, m] = keep.tile([P, D_IN], F32, name="result%d_%d" % (k, m))
                emptied[k, m] = 0
            dst = result[k, m][:, half_cols(n)]
            if who == "A":
                nc.scalar.mul(out=dst, in_=acc[k, m, n][:], mul=-1.0)
            elif who == "V":
                nc.vector.tensor_scalar_mul(out=dst, in0=acc[k, m, n][:], scalar1=-1.0)
            else:
                nc.any.tensor_scalar_mul(out=dst, in0=acc[k, m, n][:], scalar1=-1.0)
            emptied[k, m] = emptied[k, m] + 1
            row0 = c0 + m * M_TILE
            store_engine = nc.gpsimd if (k, m) in GPSIMD_STORES else nc.sync
            if (k, m) in SPLIT_STORES:
                store_engine.dma_start(out=out[row0 : row0 + M_TILE, half_cols(n)], in_=dst)
            elif emptied[k, m] == N_HALVES:
                store_engine.dma_start(out=out[row0 : row0 + M_TILE, :], in_=result[k, m][:])

        for (tensor, c0, w, queue) in LOADS:
            load(tensor, c0, w, queue)

        for token in ORDER.split():
            op = token[0]
            if op == "G":
                gate(int(token[1]))
            elif op == "X":
                x_copy(int(token[1]))
            elif op == "W":
                x_copy_on_scalar(int(token[1]))
            elif op == "Y":
                x_quant(int(token[1]))
            elif op == "S":
                first_product(int(token[1]))
            elif op == "T":
                second_product(int(token[1]))
            elif op == "Q":
                quant(int(token[1]))
            elif op == "M":
                multiply(int(token[1]))
            else:
                empty(op, int(token[1]), int(token[2]), int(token[3]))
